import numpy as np
import ml_dtypes


def mxq(x, axis, fmt="e4m3"):
    dtype, down = {"e4m3": (ml_dtypes.float8_e4m3fn, 7), "e5m2": (ml_dtypes.float8_e5m2, 14)}[fmt]
    v = np.moveaxis(np.asarray(x, np.float32).astype(ml_dtypes.bfloat16).astype(np.float64), axis, -1)
    blocks = v.reshape(v.shape[:-1] + (-1, 32))
    amax = np.abs(blocks).max(-1, keepdims=True)
    byte = np.maximum(np.where(amax > 0, np.frexp(amax)[1] - 1 + 127, 0) - down, 1)
    scale = np.exp2(byte - 127.0)
    codes = (blocks / scale).astype(np.float32).astype(dtype).astype(np.float64)
    return np.moveaxis((codes * scale).reshape(v.shape), -1, axis)


WIDE = False


def mx_kscale(k):
    if not WIDE:
        return np.ones(k)
    levels = np.array([10, -10, 5, -5, 0])
    if k % 512:
        return np.exp2(np.random.permutation(np.resize(levels, k // 32))).repeat(32)
    a = np.empty((k // 512, 16))
    for p in range(k // 512):
        a[p, :8] = np.random.permutation(np.resize(levels, 8))
        for g in range(8):
            far = levels[np.abs(levels - a[p, g]) >= 10]
            a[p, g + 8] = far[np.random.randint(len(far))]
    return np.exp2(a.ravel()).repeat(32)


BF16 = ml_dtypes.bfloat16


def bf(x):
    return np.asarray(x, np.float32).astype(BF16)


def f64(x):
    return np.asarray(x).astype(np.float64)


E2M1 = np.array([0.0, 0.5, 1.0, 1.5, 2.0, 3.0, 4.0, 6.0, -0.0, -0.5, -1.0, -1.5, -2.0, -3.0, -4.0, -6.0])


def pack_weight(w, fmt):
    k, n = w.shape
    w = f64(bf(w)).reshape(k // 32, 32, n)
    amax = np.abs(w).max(1)
    if fmt == "e4m3":
        byte = np.frexp(amax)[1] - 1 + 127 - 7
    else:
        mant, ex = np.frexp(amax / 6.0)
        byte = np.where(mant > 0.5, ex, ex - 1) + 127
    byte = np.clip(np.where(amax > 0, byte, 1), 1, 254)
    scaled = (w * np.exp2(127.0 - byte)[:, None, :]).reshape(k, n).astype(np.float32)
    by_word = np.ascontiguousarray(scaled.reshape(k // 512, 128, 4, n).transpose(0, 1, 3, 2))
    if fmt == "e4m3":
        words = by_word.astype(ml_dtypes.float8_e4m3fn).view(np.uint8)
    else:
        c = by_word.astype(ml_dtypes.float4_e2m1fn).view(np.uint8) & 0xF
        words = c[..., 0::2] | (c[..., 1::2] << 4)
    return np.ascontiguousarray(words), np.ascontiguousarray(byte.astype(np.uint8).reshape(k // 512, 16, n))


def unpack_weight(words, scales, fmt):
    g, p, n, _ = words.shape
    if fmt == "e4m3":
        vals = np.ascontiguousarray(words).view(ml_dtypes.float8_e4m3fn).astype(np.float64)
    else:
        nib = np.empty((g, p, n, 4), np.uint8)
        nib[..., 0::2] = words & 0xF
        nib[..., 1::2] = words >> 4
        vals = E2M1[nib]
    vals = vals * np.repeat(np.exp2(scales.astype(np.float64) - 127.0), 8, axis=1)[..., None]
    return vals.transpose(0, 1, 3, 2).reshape(g * 512, n)


B, IM, HID, L = 1024, 1024, 4096, 128


def relu(v):
    return np.maximum(v, 0.0)


def draw0():
    s, t = mx_kscale(IM), mx_kscale(HID)
    x = bf(np.random.random((B, IM)) * s)
    eps = bf(np.random.standard_normal((B, L)))
    W11_words, W11_scales = pack_weight(np.random.standard_normal((IM, HID)) * np.sqrt(3.0 / IM) / s[:, None] * t, "e4m3")
    b11 = bf(np.random.standard_normal(HID) * 0.2 * t)
    W31_words, W31_scales = pack_weight(np.random.standard_normal((HID, L)) * np.sqrt(2.0 / HID) / t[:, None], "e4m3")
    b31 = bf(np.random.standard_normal(L) * 0.2)
    W32_words, W32_scales = pack_weight(np.random.standard_normal((HID, L)) * np.sqrt(2.0 / HID) / t[:, None], "e4m3")
    b32 = bf(np.random.standard_normal(L) * 0.2)
    return {"x": x,
            "eps": eps,
            "W11_words": W11_words,
            "W11_scales": W11_scales,
            "b11": b11,
            "W31_words": W31_words,
            "W31_scales": W31_scales,
            "b31": b31,
            "W32_words": W32_words,
            "W32_scales": W32_scales,
            "b32": b32}


def core(x, eps, W11_words, W11_scales, b11, W31_words, W31_scales, b31, W32_words, W32_scales, b32):
    enc = relu((mxq(f64(x), 1, "e4m3") @ unpack_weight(W11_words, W11_scales, "e4m3")) + f64(b11))
    encq = mxq(enc, 1, "e4m3")
    mu = relu((encq @ unpack_weight(W31_words, W31_scales, "e4m3")) + f64(b31))
    sigma = relu((encq @ unpack_weight(W32_words, W32_scales, "e4m3")) + f64(b32))
    z = f64(eps) * sigma + mu
    return mu, sigma, z


def e4m3fn_bytes(y):
    return np.clip(np.asarray(y, np.float64), -448.0, 448.0).astype(np.float32).astype(ml_dtypes.float8_e4m3fn).view(np.uint8)


def e4m3fn_values(b):
    return np.asarray(b, np.uint8).view(ml_dtypes.float8_e4m3fn).astype(np.float64)


def setup_inputs():
    d = draw0()
    x0 = np.asarray(d['x']).astype(np.float64)
    s = (np.max(np.abs(x0), axis=(0,), keepdims=True) / 448.0).astype(np.float32)
    out = {}
    for k, v in d.items():
        if k == 'x':
            out['x_bytes'] = e4m3fn_bytes(x0 / s.astype(np.float64))
            out['x_scale'] = s
        else:
            out[k] = v
    return out


def reference(x_bytes, x_scale, eps, W11_words, W11_scales, b11, W31_words, W31_scales, b31, W32_words, W32_scales, b32):
    return core(e4m3fn_values(x_bytes) * x_scale.astype(np.float64), eps, W11_words, W11_scales, b11, W31_words, W31_scales, b31, W32_words, W32_scales, b32)

@@ -1,0 +1,469 @@
+from contextlib import ExitStack
+
+import concourse.mybir as mybir
+from concourse.masks import make_identity
+
+F32 = mybir.dt.float32
+BF16 = mybir.dt.bfloat16
+I32 = mybir.dt.int32
+U32 = mybir.dt.uint32
+U8 = mybir.dt.uint8
+FP8 = mybir.dt.float8_e4m3fn
+FP8X4 = mybir.dt.float8_e4m3fn_x4
+ACT = mybir.ActivationFunctionType
+ALU = mybir.AluOpType
+
+P = 128
+PACK = 4
+TOKENS, K1, HID, LATENT = 1024, 1024, 4096, 128
+FLOPS = 2 * TOKENS * K1 * HID + 2 * TOKENS * HID * 2 * LATENT
+
+K_PASS = 512
+X_PASSES = K1 // K_PASS
+GROUPS = HID // K_PASS
+CHUNK = 256
+CHUNKS = TOKENS // CHUNK
+TILES = CHUNK // P
+GROUP_ORDER = (0, 4, 1, 5, 2, 6, 3, 7)
+
+UNITS = (
+    [(0, 2, i) for i in range(3)]
+    + [(2, 2, i) for i in range(3)]
+    + [(0, 4, i) for i in range(3, 8)]
+    + [(4, 2, i) for i in range(3)]
+    + [(6, 2, i) for i in range(3)]
+    + [(4, 4, i) for i in range(3, 7)]
+    + [(4, 2, 7), (6, 1, 7), (7, 1, 7)]
+)
+LAGS = (3, 4, 7)
+LATE_LAGS = (1, 1, 2)
+LATE = 19
+PAIRED = frozenset(range(14, 24))
+X_STEP = (0, 1, 9, 11)
+CAST_ON_VECTOR = ()
+PERM_AHEAD = 2
+TAIL_VECTOR = (21, 22, 23)
+RELU_ON_GPSIMD = (0, 1, 2)
+SHARED = ()
+
+
+def tile_mae_pa_w8_kernel(
+    tc, x_bytes, x_scale, eps, w11_words, w11_scales, b11,
+    w31_words, w31_scales, b31, w32_words, w32_scales, b32,
+    out_mu, out_sigma, out_z,
+):
+    nc = tc.nc
+    with ExitStack() as ctx:
+        keep = ctx.enter_context(tc.tile_pool(name="keep", bufs=1))
+        work = ctx.enter_context(tc.tile_pool(name="work", bufs=2))
+        psum = ctx.enter_context(tc.psum_pool(name="psum", bufs=1))
+        ctx.enter_context(tc.manual_schedule())
+
+        warm = keep.tile([P, 1], F32, name="warm")
+        nc.vector.memset(warm[:], 0.0)
+        nc.scalar.activation(out=warm[:], in_=warm[:], func=ACT.Relu)
+        w11s_raw = keep.tile([P, HID // 2], U8, name="w11s_raw", align_bytes=64)
+        w11s = keep.tile([P, HID // 2], U8, name="w11s", align_bytes=64)
+        nc.vector.memset(w11s_raw[:].bitcast(I32), 0)
+        small = keep.tile([P, 768], BF16, name="small", align_bytes=64)
+        nc.vector.memset(small[:], 0.0)
+        ones = keep.tile([P, P], BF16, name="ones", align_bytes=64)
+        nc.vector.memset(ones[:], 1.0)
+        ident = keep.tile([P, P], F32, name="ident", align_bytes=64)
+        make_identity(nc, ident[:])
+        ident_bf = keep.tile([P, P], BF16, name="ident_bf", align_bytes=64)
+        make_identity(nc, ident_bf[:])
+        w3s = keep.tile([P, GROUPS, 2 * LATENT], U8, name="w3s", align_bytes=64)
+        nc.gpsimd.memset(w3s[:].rearrange("p g n -> p (g n)").bitcast(I32), 0)
+
+        x_raw = []
+        for c in range(CHUNKS):
+            xr = keep.tile([P, TILES * K1], U8, name=f"x_raw{c}", align_bytes=64)
+            x_raw.append(xr)
+
+        def load_x(c):
+            nc.sync.dma_start(
+                out=x_raw[c][:],
+                in_=x_bytes[c * CHUNK : (c + 1) * CHUNK, :].rearrange("(p a) k -> p (a k)", a=TILES),
+            )
+
+        w11_raw = {}
+        w11 = {}
+
+        def load_w11(i):
+            gid = GROUP_ORDER[i]
+            raw = work.tile([P, X_PASSES, K_PASS], I32, name="w11_raw", bufs=8, align_bytes=64)
+            w11_raw[i] = raw
+            nc.sync.dma_start(
+                out=raw[:],
+                in_=w11_words[:, :, gid * K_PASS : (gid + 1) * K_PASS, :]
+                .rearrange("g p n t -> p g (n t)")
+                .bitcast(I32),
+            )
+
+        scale_col = keep.tile([P, X_PASSES * PACK], F32, name="scale_col", align_bytes=64)
+        nc.scalar.dma_start(
+            out=scale_col[:].rearrange("p (g t) -> p g t", t=PACK),
+            in_=x_scale.rearrange("o (g p t) -> p (o g) t", p=P, t=PACK),
+        )
+        load_x(0)
+        load_w11(0)
+        for h in range(2):
+            for q in range(4):
+                nc.sync.dma_start(
+                    out=w11s_raw[32 * q + 8 * h : 32 * q + 8 * h + 8, :].bitcast(I32),
+                    in_=w11_scales[:, 4 * q : 4 * q + 4, h * 2048 : (h + 1) * 2048].bitcast(I32),
+                )
+        nc.scalar.dma_start(out=small[0:GROUPS, 0:K_PASS], in_=b11.rearrange("(g n) -> g n", g=GROUPS))
+        nc.scalar.dma_start(out=small[0:1, 512:640], in_=b31.rearrange("(o n) -> o n", o=1))
+        nc.scalar.dma_start(out=small[0:1, 640:768], in_=b32.rearrange("(o n) -> o n", o=1))
+        load_x(1)
+        load_w11(1)
+        load_w11(2)
+        load_w11(3)
+        load_w11(4)
+        w3 = keep.tile([P, GROUPS, 2 * LATENT], I32, name="w3", align_bytes=64)
+        for j, (words, scales) in enumerate(((w31_words, w31_scales), (w32_words, w32_scales))):
+            cols = slice(j * LATENT, (j + 1) * LATENT)
+            for q in range(4):
+                nc.sync.dma_start(
+                    out=w3s[32 * q : 32 * q + 4, :, cols].bitcast(I32),
+                    in_=scales[:, 4 * q : 4 * q + 4, :].rearrange("g q n -> q g n").bitcast(I32),
+                )
+        for j, words in enumerate((w31_words, w32_words)):
+            nc.sync.dma_start(
+                out=w3[:, :, j * LATENT : (j + 1) * LATENT],
+                in_=words.rearrange("g p n t -> p g (n t)").bitcast(I32),
+            )
+        load_x(2)
+        load_w11(5)
+        load_w11(6)
+        load_w11(7)
+        load_x(3)
+        noise = keep.tile([P, CHUNKS, TILES, LATENT], BF16, name="noise", align_bytes=64)
+        for c in range(CHUNKS):
+            nc.sync.dma_start(
+                out=noise[:, c, :, :],
+                in_=eps[c * CHUNK : (c + 1) * CHUNK, :].rearrange("(p a) n -> p a n", a=TILES),
+            )
+
+        xq = []
+        xs = []
+        for s in range(CHUNKS // 2):
+            xq_s = keep.tile([P, X_PASSES, 2 * CHUNK], U32, name=f"xq{s}", align_bytes=64)
+            xs_s = keep.tile([P, X_PASSES, 2 * CHUNK], U8, name=f"xs{s}", align_bytes=64)
+            xq.append(xq_s)
+            xs.append(xs_s)
+        x_wide = {}
+        x_bank = {}
+        x_grouped = {}
+
+        def widen_tile(c):
+            xw = work.tile([P, TILES, K1], BF16, name="x_wide", bufs=2, align_bytes=64)
+            x_wide[c] = xw
+
+        def widen_first(c):
+            widen_tile(c)
+            for a in range(TILES):
+                for g, copy in ((0, nc.vector.tensor_copy), (1, nc.scalar.copy)):
+                    lo = a * K1 + g * K_PASS
+                    copy(
+                        out=x_wide[c][:, a, g * K_PASS : (g + 1) * K_PASS],
+                        in_=x_raw[c][:, lo : lo + K_PASS].bitcast(FP8),
+                    )
+
+        def widen(c, a):
+            copy = nc.vector.tensor_copy if c in CAST_ON_VECTOR else nc.scalar.copy
+            copy(out=x_wide[c][:, a, :], in_=x_raw[c][:, a * K1 : (a + 1) * K1].bitcast(FP8))
+
+        def turn_x(c, g):
+            words = x_wide[c][:].rearrange("p a k -> p (a k)").bitcast(F32)
+            per_bank = 1 if (c, g) in SHARED else 2
+            x_bank[c, g] = []
+            for u0 in range(0, 2, per_bank):
+                bank = psum.tile([P, per_bank, CHUNK], F32, name="bank", bufs=4)
+                x_bank[c, g].append(bank)
+                for a in range(TILES):
+                    for u in range(u0, u0 + per_bank):
+                        lo = a * (K1 // 2) + g * (K_PASS // 2)
+                        nc.tensor.transpose(
+                            bank[:, u - u0, a * P : (a + 1) * P],
+                            words[:, lo + u : lo + K_PASS // 2 : 2],
+                            ident[:],
+                        )
+
+        def bank_values(bank, pairs):
+            return bank[:].rearrange("p u r -> p (u r)").bitcast(BF16).rearrange("p (u r e) -> p r u e", u=pairs, e=2)
+
+        def scale_x(c, g):
+            grouped = work.tile([P, CHUNK, PACK], BF16, name="x_grouped", bufs=4, align_bytes=64)
+            x_grouped[c, g] = grouped
+            pairs = 1 if (c, g) in SHARED else 2
+            slots = grouped[:].rearrange("p r (u e) -> p r u e", u=2)
+            factor = scale_col[:, g * PACK : g * PACK + 2 * pairs].rearrange("p (u e) -> p u e", u=pairs)
+            nc.vector.tensor_tensor(
+                out=slots[:, :, 0:pairs, :],
+                in0=bank_values(x_bank[c, g][0], pairs),
+                in1=factor.unsqueeze(1).to_broadcast([P, CHUNK, pairs, 2]),
+                op=ALU.mult,
+            )
+            if pairs == 1:
+                for e in range(2):
+                    nc.scalar.activation(
+                        out=slots[:, :, 1, e],
+                        in_=bank_values(x_bank[c, g][1], 1)[:, :, 0, e],
+                        func=ACT.Copy,
+                        scale=scale_col[:, g * PACK + 2 + e : g * PACK + 3 + e],
+                    )
+
+        def quantize_x(c, g):
+            cols = slice((c % 2) * CHUNK, (c % 2 + 1) * CHUNK)
+            nc.vector.quantize_mx(
+                out=xq[c // 2][:, g, cols].bitcast(FP8X4),
+                scales=xs[c // 2][:, g, cols],
+                in_=x_grouped[c, g][:].rearrange("p r t -> p (r t)"),
+            )
+
+        def permute_w11(i):
+            codes = keep.tile([P, X_PASSES, K_PASS], I32, name=f"w11_{i}", align_bytes=64)
+            w11[i] = codes
+            nc.vector.tensor_copy(
+                out=codes[:].rearrange("p g (t m) -> p g t m", t=PACK),
+                in_=w11_raw[i][:].rearrange("p g (m t) -> p g t m", t=PACK),
+            )
+
+        def permute_scales(b, engine):
+            cols = slice(b * K_PASS, (b + 1) * K_PASS)
+            engine.tensor_copy(
+                out=w11s[:, cols].rearrange("p (t m) -> p m t", t=PACK),
+                in_=w11s_raw[:, cols].rearrange("p (m t) -> p m t", t=PACK),
+            )
+
+        bias11 = keep.tile([P, GROUPS, PACK], F32, name="bias11", align_bytes=64)
+        bias3 = keep.tile([P, 2 * LATENT], F32, name="bias3", align_bytes=64)
+
+        def spread_biases():
+            turned = psum.tile([P, PACK, P], BF16, name="bank", bufs=4)
+            for t in range(PACK):
+                nc.tensor.transpose(turned[:, t, :], small[:, t : K_PASS : PACK], ident_bf[:])
+            nc.scalar.copy(out=bias11[:], in_=turned[:, :, 0:GROUPS].rearrange("p t g -> p g t"))
+            spread = psum.tile([P, 2, CHUNK], F32, name="bank", bufs=4)
+            nc.tensor.matmul(spread[:, 0, :], lhsT=ones[:], rhs=small[:, 512:768], start=True, stop=True)
+            nc.scalar.copy(out=bias3[:], in_=spread[:, 0, :])
+
+        enc = {}
+        grouped_enc = {}
+        codes_enc = {}
+        acc = {}
+
+        def paired(u):
+            return u in PAIRED
+
+        def unit_cols(u):
+            first, tiles, i = UNITS[u]
+            lo = (first % 4) * P
+            return slice(lo, lo + tiles * P)
+
+        def multiply1(u, fillers=()):
+            fillers = list(fillers)
+            first, tiles, i = UNITS[u]
+            s = first // 4
+            n = tiles * P
+            cols = unit_cols(u)
+            gid = GROUP_ORDER[i]
+            e = work.tile([P, PACK * n], BF16, name="enc", bufs=8, align_bytes=64)
+            enc[u] = e
+            if paired(u):
+                slots = e[:].rearrange("p (h n l) -> p h l n", h=2, l=2)
+            else:
+                slots = e[:].rearrange("p (h l n) -> p h l n", h=2, l=2)
+            per_bank = min(512 // n, 2)
+            for t in range(PACK):
+                if t % per_bank == 0:
+                    bank = psum.tile([P, per_bank, n], F32, name="bank", bufs=4)
+                for g in range(X_PASSES):
+                    plane = 8 * (gid // 4) + 4 * g
+                    sc = (gid % 4) * K_PASS + t * P
+                    nc.tensor.matmul_mx(
+                        out=bank[:, t % per_bank, :],
+                        lhsT=w11[i][:, g, t * P : (t + 1) * P].bitcast(FP8X4),
+                        lhsT_scale=w11s[plane:P, sc : sc + P],
+                        rhs=xq[s][:, g, cols].bitcast(FP8X4),
+                        rhs_scale=xs[s][:, g, cols],
+                        start=(g == 0),
+                        stop=(g == X_PASSES - 1),
+                    )
+                if t % per_bank == per_bank - 1:
+                    for b in range(per_bank):
+                        v = t - per_bank + 1 + b
+                        if u in TAIL_VECTOR and t == PACK - 1:
+                            nc.vector.tensor_scalar(
+                                out=slots[:, v // 2, v % 2, :],
+                                in0=bank[:, b, :],
+                                scalar1=bias11[:, gid, v : v + 1],
+                                scalar2=0.0,
+                                op0=ALU.add,
+                                op1=ALU.max,
+                            )
+                            continue
+                        nc.scalar.activation(
+                            out=slots[:, v // 2, v % 2, :],
+                            in_=bank[:, b, :],
+                            func=ACT.Relu,
+                            bias=bias11[:, gid, v : v + 1],
+                        )
+                    banks_left = (PACK - 1 - t) // per_bank
+                    while len(fillers) > banks_left * ((len(fillers) + banks_left) // (banks_left + 1)):
+                        fillers.pop(0)()
+            for filler in fillers:
+                filler()
+
+        def interleave(u):
+            n = UNITS[u][1] * P
+            grouped = work.tile([P, n, PACK], BF16, name="enc_grouped", bufs=3, align_bytes=64)
+            grouped_enc[u] = grouped
+            if paired(u):
+                nc.vector.tensor_copy(
+                    out=grouped[:].rearrange("p n t -> p (n t)").bitcast(F32),
+                    in_=enc[u][:].bitcast(F32).rearrange("p (h n) -> p n h", h=2),
+                )
+            else:
+                nc.vector.tensor_copy(
+                    out=grouped[:].rearrange("p (c i) t -> p c t i", i=4),
+                    in_=enc[u][:].rearrange("p (t c i) -> p c t i", t=PACK, i=4),
+                )
+
+        def quantize(u):
+            n = UNITS[u][1] * P
+            codes = work.tile([P, n], U32, name="enc_codes", bufs=7, align_bytes=64)
+            planes = work.tile([P, n], U8, name="enc_planes", bufs=7, align_bytes=64)
+            codes_enc[u] = (codes, planes)
+            nc.vector.quantize_mx(
+                out=codes[:].bitcast(FP8X4),
+                scales=planes[:],
+                in_=grouped_enc[u][:].rearrange("p r t -> p (r t)"),
+            )
+
+        def multiply2(u):
+            return [lambda b=b: multiply2_tile(u, b) for b in range(UNITS[u][1])]
+
+        def multiply2_tile(u, b):
+            first, tiles, i = UNITS[u]
+            tile = first + b
+            gid = GROUP_ORDER[i]
+            codes, planes = codes_enc[u]
+            if i == 0:
+                sums = psum.tile([P, 2 * LATENT], F32, name=f"sums{tile % 4}", bufs=1)
+                acc[tile] = sums
+            cols = slice(b * P, (b + 1) * P)
+            nc.tensor.matmul_mx(
+                out=acc[tile][:],
+                lhsT=codes[:, cols].bitcast(FP8X4),
+                lhsT_scale=planes[:, cols],
+                rhs=w3[:, gid, :].bitcast(FP8X4),
+                rhs_scale=w3s[:, gid, :],
+                start=(i == 0),
+                stop=(i == GROUPS - 1),
+            )
+            if i == GROUPS - 1 and b == tiles - 1:
+                ready.append((first, tiles))
+
+        def finish(first, tiles):
+            for lo in range(first, first + tiles, TILES):
+                finish_tiles(lo // TILES, lo % TILES, min(TILES, tiles))
+
+        def finish_tiles(c, a0, tiles):
+            pre = work.tile([P, tiles, 2, LATENT], F32, name="pre", bufs=3, align_bytes=64)
+            both = work.tile([P, 2, tiles, LATENT], F32, name="both", bufs=3, align_bytes=64)
+            z = work.tile([P, tiles, LATENT], F32, name="z", bufs=3, align_bytes=64)
+            for a in range(tiles):
+                nc.vector.tensor_tensor(
+                    out=pre[:, a, :, :].rearrange("p w n -> p (w n)"),
+                    in0=acc[c * TILES + a0 + a][:],
+                    in1=bias3[:],
+                    op=ALU.add,
+                )
+            if c in RELU_ON_GPSIMD:
+                for a in range(tiles):
+                    nc.gpsimd.tensor_scalar(
+                        out=both[:, :, a, :], in0=pre[:, a, :, :], scalar1=0.0, scalar2=0.0, op0=ALU.max, op1=ALU.add
+                    )
+            else:
+                nc.scalar.activation(out=both[:].rearrange("p w a n -> p a w n"), in_=pre[:], func=ACT.Relu)
+            nc.vector.scalar_tensor_tensor(
+                out=z[:], in0=pre[:, :, 1, :], scalar=0.0, in1=noise[:, c, a0 : a0 + tiles, :], op0=ALU.max, op1=ALU.mult
+            )
+            nc.vector.scalar_tensor_tensor(
+                out=z[:], in0=pre[:, :, 0, :], scalar=0.0, in1=z[:], op0=ALU.max, op1=ALU.add
+            )
+            rows = slice(c * CHUNK, (c + 1) * CHUNK)
+            for dst, src in ((out_mu, both[:, 0, :, :]), (out_sigma, both[:, 1, :, :]), (out_z, z[:])):
+                nc.sync.dma_start(
+                    out=dst[rows, :].rearrange("(p a) n -> p a n", a=TILES)[:, a0 : a0 + tiles, :], in_=src
+                )
+
+        widen_first(0)
+        turn_x(0, 0)
+        turn_x(0, 1)
+        permute_w11(0)
+        scale_x(0, 0)
+        scale_x(0, 1)
+        spread_biases()
+        widen_tile(1)
+        widen(1, 0)
+        widen(1, 1)
+        quantize_x(0, 0)
+        quantize_x(0, 1)
+        permute_scales(0, nc.vector)
+        permute_w11(1)
+        permute_scales(1, nc.vector)
+        before = {}
+        def put(k, item):
+            before.setdefault(k, []).append(item)
+
+        for c in (1, 2, 3):
+            k = X_STEP[c]
+            if c > 1:
+                put(k - 2, lambda c=c: widen_tile(c))
+                put(k - 2, lambda c=c: widen(c, 0))
+                put(k - 1, lambda c=c: widen(c, 1))
+            for g in range(X_PASSES):
+                put(k, lambda c=c, g=g: turn_x(c, g))
+            for g in range(X_PASSES):
+                put(k, lambda c=c, g=g: scale_x(c, g))
+            for g in range(X_PASSES):
+                put(k + 1, lambda c=c, g=g: quantize_x(c, g))
+        first_use = {}
+        for u, (first, tiles, i) in enumerate(UNITS):
+            first_use.setdefault(i, u)
+        for i in range(2, GROUPS):
+            put(first_use[i] - PERM_AHEAD, lambda i=i: permute_w11(i))
+            if i in (2, 3):
+                put(first_use[i] - PERM_AHEAD, lambda i=i: permute_scales(i, nc.vector))
+        ready = []
+        made = [0, 0, 0]
+        for k in range(len(UNITS) + 4):
+            lags = LAGS if k < LATE else LATE_LAGS
+            for work_item in before.get(k, []):
+                work_item()
+            while made[0] < len(UNITS) and made[0] <= k - lags[0]:
+                interleave(made[0])
+                made[0] += 1
+                if made[1] < len(UNITS) and made[1] <= k - lags[1]:
+                    quantize(made[1])
+                    made[1] += 1
+            while made[1] < len(UNITS) and made[1] <= k - lags[1]:
+                quantize(made[1])
+                made[1] += 1
+            fillers = []
+            while made[2] < len(UNITS) and made[2] <= k - lags[2]:
+                fillers += multiply2(made[2])
+                made[2] += 1
+            if k < len(UNITS):
+                multiply1(k, fillers)
+            else:
+                for filler in fillers:
+                    filler()
+            for first, tiles in ready:
+                finish(first, tiles)
+            ready.clear()

@@ -35,16 +35,17 @@ UNITS = (
     + [(4, 4, i) for i in range(3, 7)]
     + [(4, 2, 7), (6, 1, 7), (7, 1, 7)]
 )
-LAGS = (3, 4, 7)
-LATE_LAGS = (1, 1, 2)
-LATE = 19
-PAIRED = frozenset(range(14, 24))
-X_STEP = (0, 1, 9, 11)
+LAGS = (2, 3, 6)
+LATE_LAGS = (1, 2, 3)
+LATE = 24
+PAIRED = frozenset((21, 22, 23))
+X_STEP = (0, 1, 7, 10)
 CAST_ON_VECTOR = ()
 PERM_AHEAD = 2
-TAIL_VECTOR = (21, 22, 23)
+TAIL_VECTOR = ()
 RELU_ON_GPSIMD = (0, 1, 2)
 SHARED = ()
+ON_SCALAR = frozenset()
 
 
 def tile_mae_pa_w8_kernel(
@@ -107,23 +108,22 @@ def tile_mae_pa_w8_kernel(
             in_=x_scale.rearrange("o (g p t) -> p (o g) t", p=P, t=PACK),
         )
         load_x(0)
-        load_w11(0)
         for h in range(2):
             for q in range(4):
                 nc.sync.dma_start(
                     out=w11s_raw[32 * q + 8 * h : 32 * q + 8 * h + 8, :].bitcast(I32),
                     in_=w11_scales[:, 4 * q : 4 * q + 4, h * 2048 : (h + 1) * 2048].bitcast(I32),
                 )
-        nc.scalar.dma_start(out=small[0:GROUPS, 0:K_PASS], in_=b11.rearrange("(g n) -> g n", g=GROUPS))
-        nc.scalar.dma_start(out=small[0:1, 512:640], in_=b31.rearrange("(o n) -> o n", o=1))
-        nc.scalar.dma_start(out=small[0:1, 640:768], in_=b32.rearrange("(o n) -> o n", o=1))
-        load_x(1)
+        load_w11(0)
+        nc.sync.dma_start(out=small[0:GROUPS, 0:K_PASS], in_=b11.rearrange("(g n) -> g n", g=GROUPS))
         load_w11(1)
+        load_x(1)
         load_w11(2)
         load_w11(3)
-        load_w11(4)
+        nc.sync.dma_start(out=small[0:1, 512:640], in_=b31.rearrange("(o n) -> o n", o=1))
+        nc.sync.dma_start(out=small[0:1, 640:768], in_=b32.rearrange("(o n) -> o n", o=1))
         w3 = keep.tile([P, GROUPS, 2 * LATENT], I32, name="w3", align_bytes=64)
-        for j, (words, scales) in enumerate(((w31_words, w31_scales), (w32_words, w32_scales))):
+        for j, scales in enumerate((w31_scales, w32_scales)):
             cols = slice(j * LATENT, (j + 1) * LATENT)
             for q in range(4):
                 nc.sync.dma_start(
@@ -135,11 +135,12 @@ def tile_mae_pa_w8_kernel(
                 out=w3[:, :, j * LATENT : (j + 1) * LATENT],
                 in_=words.rearrange("g p n t -> p g (n t)").bitcast(I32),
             )
+        load_w11(4)
         load_x(2)
         load_w11(5)
+        load_x(3)
         load_w11(6)
         load_w11(7)
-        load_x(3)
         noise = keep.tile([P, CHUNKS, TILES, LATENT], BF16, name="noise", align_bytes=64)
         for c in range(CHUNKS):
             nc.sync.dma_start(
@@ -225,11 +226,11 @@ def tile_mae_pa_w8_kernel(
             )
 
         def permute_w11(i):
-            codes = keep.tile([P, X_PASSES, K_PASS], I32, name=f"w11_{i}", align_bytes=64)
+            codes = keep.tile([P, PACK, X_PASSES, P], I32, name=f"w11_{i}", align_bytes=64)
             w11[i] = codes
             nc.vector.tensor_copy(
-                out=codes[:].rearrange("p g (t m) -> p g t m", t=PACK),
-                in_=w11_raw[i][:].rearrange("p g (m t) -> p g t m", t=PACK),
+                out=codes[:].rearrange("p t g (c i) -> p (g c) t i", i=4),
+                in_=w11_raw[i][:].rearrange("p g (c i t) -> p (g c) t i", i=4, t=PACK),
             )
 
         def permute_scales(b, engine):
@@ -247,6 +248,8 @@ def tile_mae_pa_w8_kernel(
             for t in range(PACK):
                 nc.tensor.transpose(turned[:, t, :], small[:, t : K_PASS : PACK], ident_bf[:])
             nc.scalar.copy(out=bias11[:], in_=turned[:, :, 0:GROUPS].rearrange("p t g -> p g t"))
+
+        def spread_last_biases():
             spread = psum.tile([P, 2, CHUNK], F32, name="bank", bufs=4)
             nc.tensor.matmul(spread[:, 0, :], lhsT=ones[:], rhs=small[:, 512:768], start=True, stop=True)
             nc.scalar.copy(out=bias3[:], in_=spread[:, 0, :])
@@ -286,7 +289,7 @@ def tile_mae_pa_w8_kernel(
                     sc = (gid % 4) * K_PASS + t * P
                     nc.tensor.matmul_mx(
                         out=bank[:, t % per_bank, :],
-                        lhsT=w11[i][:, g, t * P : (t + 1) * P].bitcast(FP8X4),
+                        lhsT=w11[i][:, t, g, :].bitcast(FP8X4),
                         lhsT_scale=w11s[plane:P, sc : sc + P],
                         rhs=xq[s][:, g, cols].bitcast(FP8X4),
                         rhs_scale=xs[s][:, g, cols],
@@ -328,7 +331,8 @@ def tile_mae_pa_w8_kernel(
                     in_=enc[u][:].bitcast(F32).rearrange("p (h n) -> p n h", h=2),
                 )
             else:
-                nc.vector.tensor_copy(
+                copy = nc.scalar.copy if u in ON_SCALAR else nc.vector.tensor_copy
+                copy(
                     out=grouped[:].rearrange("p (c i) t -> p c t i", i=4),
                     in_=enc[u][:].rearrange("p (t c i) -> p c t i", t=PACK, i=4),
                 )
@@ -368,6 +372,8 @@ def tile_mae_pa_w8_kernel(
             if i == GROUPS - 1 and b == tiles - 1:
                 ready.append((first, tiles))
 
+        later = []
+
         def finish(first, tiles):
             for lo in range(first, first + tiles, TILES):
                 finish_tiles(lo // TILES, lo % TILES, min(TILES, tiles))
@@ -390,22 +396,31 @@ def tile_mae_pa_w8_kernel(
                     )
             else:
                 nc.scalar.activation(out=both[:].rearrange("p w a n -> p a w n"), in_=pre[:], func=ACT.Relu)
-            nc.vector.scalar_tensor_tensor(
-                out=z[:], in0=pre[:, :, 1, :], scalar=0.0, in1=noise[:, c, a0 : a0 + tiles, :], op0=ALU.max, op1=ALU.mult
-            )
-            nc.vector.scalar_tensor_tensor(
-                out=z[:], in0=pre[:, :, 0, :], scalar=0.0, in1=z[:], op0=ALU.max, op1=ALU.add
-            )
+            def weigh():
+                nc.vector.scalar_tensor_tensor(
+                    out=z[:], in0=pre[:, :, 1, :], scalar=0.0, in1=noise[:, c, a0 : a0 + tiles, :], op0=ALU.max, op1=ALU.mult
+                )
+
+            def shift():
+                nc.vector.scalar_tensor_tensor(
+                    out=z[:], in0=pre[:, :, 0, :], scalar=0.0, in1=z[:], op0=ALU.max, op1=ALU.add
+                )
+                store(out_z, z[:])
+
             rows = slice(c * CHUNK, (c + 1) * CHUNK)
-            for dst, src in ((out_mu, both[:, 0, :, :]), (out_sigma, both[:, 1, :, :]), (out_z, z[:])):
+
+            def store(dst, src):
                 nc.sync.dma_start(
                     out=dst[rows, :].rearrange("(p a) n -> p a n", a=TILES)[:, a0 : a0 + tiles, :], in_=src
                 )
 
+            store(out_mu, both[:, 0, :, :])
+            store(out_sigma, both[:, 1, :, :])
+            later.extend((weigh, shift))
+
         widen_first(0)
         turn_x(0, 0)
         turn_x(0, 1)
-        permute_w11(0)
         scale_x(0, 0)
         scale_x(0, 1)
         spread_biases()
@@ -414,10 +429,11 @@ def tile_mae_pa_w8_kernel(
         widen(1, 1)
         quantize_x(0, 0)
         quantize_x(0, 1)
+        permute_w11(0)
         permute_scales(0, nc.vector)
         permute_w11(1)
         permute_scales(1, nc.vector)
-        before = {}
+        before = {5: [spread_last_biases]}
         def put(k, item):
             before.setdefault(k, []).append(item)
 
@@ -446,15 +462,17 @@ def tile_mae_pa_w8_kernel(
             lags = LAGS if k < LATE else LATE_LAGS
             for work_item in before.get(k, []):
                 work_item()
-            while made[0] < len(UNITS) and made[0] <= k - lags[0]:
-                interleave(made[0])
-                made[0] += 1
+            while made[1] < len(UNITS) and made[1] <= k - lags[1] or made[0] < len(UNITS) and made[0] <= k - lags[0]:
+                if made[0] < len(UNITS) and made[0] <= k - lags[0]:
+                    interleave(made[0])
+                    made[0] += 1
+                    if later:
+                        later.pop(0)()
                 if made[1] < len(UNITS) and made[1] <= k - lags[1]:
                     quantize(made[1])
                     made[1] += 1
-            while made[1] < len(UNITS) and made[1] <= k - lags[1]:
-                quantize(made[1])
-                made[1] += 1
+                    if later:
+                        later.pop(0)()
             fillers = []
             while made[2] < len(UNITS) and made[2] <= k - lags[2]:
                 fillers += multiply2(made[2])
@@ -467,3 +485,5 @@ def tile_mae_pa_w8_kernel(
             for first, tiles in ready:
                 finish(first, tiles)
             ready.clear()
+        for work_item in later:
+            work_item()

@@ -13,45 +13,53 @@ FP8X4 = mybir.dt.float8_e4m3fn_x4
 ACT = mybir.ActivationFunctionType
 ALU = mybir.AluOpType
 
+TOKENS, PIXELS, HIDDEN, LATENT = 1024, 1024, 4096, 128
+FLOPS = 2 * TOKENS * PIXELS * HIDDEN + 2 * TOKENS * HIDDEN * 2 * LATENT
+
 P = 128
 PACK = 4
-TOKENS, K1, HID, LATENT = 1024, 1024, 4096, 128
-FLOPS = 2 * TOKENS * K1 * HID + 2 * TOKENS * HID * 2 * LATENT
-
-K_PASS = 512
-X_PASSES = K1 // K_PASS
-GROUPS = HID // K_PASS
-CHUNK = 256
+K_PASS = P * PACK
+X_PASSES = PIXELS // K_PASS
+GROUPS = HIDDEN // K_PASS
+CHUNK_TILES = 2
+CHUNK = CHUNK_TILES * P
 CHUNKS = TOKENS // CHUNK
-TILES = CHUNK // P
+HALF_TILES = 4
+BANK = 512
+
+HALF_HIDDEN = HIDDEN // 2
 GROUP_ORDER = (0, 4, 1, 5, 2, 6, 3, 7)
 
 UNITS = (
-    [(0, 2, i) for i in range(3)]
-    + [(2, 2, i) for i in range(3)]
-    + [(0, 4, i) for i in range(3, 8)]
-    + [(4, 2, i) for i in range(3)]
-    + [(6, 2, i) for i in range(3)]
-    + [(4, 4, i) for i in range(3, 7)]
-    + [(4, 2, 7), (6, 1, 7), (7, 1, 7)]
+    [(0, 2, 0), (0, 2, 1), (2, 2, 0), (2, 2, 1)]
+    + [(0, 4, i) for i in range(2, GROUPS)]
+    + [(4, 2, 0), (6, 2, 0)]
+    + [(4, 4, i) for i in range(1, GROUPS - 1)]
+    + [(4, 2, GROUPS - 1), (6, 2, GROUPS - 1)]
 )
-LAGS = (2, 3, 6)
-LATE_LAGS = (1, 2, 3)
-LATE = 24
-PAIRED = frozenset((21, 22, 23))
-X_STEP = (0, 1, 7, 10)
-CAST_ON_VECTOR = ()
-PERM_AHEAD = 2
-TAIL_VECTOR = ()
-RELU_ON_GPSIMD = (0, 1, 2)
-SHARED = ()
-ON_SCALAR = frozenset()
+INTERLEAVE_LAG, QUANTIZE_LAG, SECOND_LAG = 2, 3, 5
+X_STEP = {1: 0, 2: 6, 3: 9}
+BIAS_STEP = 5
+WARM_BEFORE, WARM_AFTER = 3, 5
 
 
 def tile_mae_pa_w8_kernel(
-    tc, x_bytes, x_scale, eps, w11_words, w11_scales, b11,
-    w31_words, w31_scales, b31, w32_words, w32_scales, b32,
-    out_mu, out_sigma, out_z,
+    tc,
+    x_bytes,
+    x_scale,
+    eps,
+    w11_words,
+    w11_scales,
+    b11,
+    w31_words,
+    w31_scales,
+    b31,
+    w32_words,
+    w32_scales,
+    b32,
+    out_mu,
+    out_sigma,
+    out_z,
 ):
     nc = tc.nc
     with ExitStack() as ctx:
@@ -60,430 +68,371 @@ def tile_mae_pa_w8_kernel(
         psum = ctx.enter_context(tc.psum_pool(name="psum", bufs=1))
         ctx.enter_context(tc.manual_schedule())
 
-        warm = keep.tile([P, 1], F32, name="warm")
-        nc.vector.memset(warm[:], 0.0)
-        nc.scalar.activation(out=warm[:], in_=warm[:], func=ACT.Relu)
-        w11s_raw = keep.tile([P, HID // 2], U8, name="w11s_raw", align_bytes=64)
-        w11s = keep.tile([P, HID // 2], U8, name="w11s", align_bytes=64)
-        nc.vector.memset(w11s_raw[:].bitcast(I32), 0)
-        small = keep.tile([P, 768], BF16, name="small", align_bytes=64)
-        nc.vector.memset(small[:], 0.0)
-        ones = keep.tile([P, P], BF16, name="ones", align_bytes=64)
+        first_act = keep.tile([P, 1], F32, name="first_act")
+        nc.vector.memset(first_act[:], 0.0)
+        nc.scalar.activation(out=first_act[:], in_=first_act[:], func=ACT.Relu)
+
+        w11_planes_raw = keep.tile([P, HALF_HIDDEN], U8, name="w11_planes_raw", align_bytes=64)
+        w11_planes = keep.tile([P, HALF_HIDDEN], U8, name="w11_planes", align_bytes=64)
+        nc.vector.memset(w11_planes_raw[:].bitcast(I32), 0)
+        bias_rows = keep.tile([P, K_PASS + 2 * LATENT], BF16, name="bias_rows", align_bytes=64)
+        nc.vector.memset(bias_rows[:], 0.0)
+        ones = keep.tile([P, 2 * LATENT], BF16, name="ones", align_bytes=64)
         nc.vector.memset(ones[:], 1.0)
         ident = keep.tile([P, P], F32, name="ident", align_bytes=64)
         make_identity(nc, ident[:])
-        ident_bf = keep.tile([P, P], BF16, name="ident_bf", align_bytes=64)
-        make_identity(nc, ident_bf[:])
-        w3s = keep.tile([P, GROUPS, 2 * LATENT], U8, name="w3s", align_bytes=64)
-        nc.gpsimd.memset(w3s[:].rearrange("p g n -> p (g n)").bitcast(I32), 0)
+        ident_bf16 = keep.tile([P, P], BF16, name="ident_bf16", align_bytes=64)
+        make_identity(nc, ident_bf16[:])
+        w3_planes = keep.tile([P, GROUPS, 2 * LATENT], U8, name="w3_planes", align_bytes=64)
+        nc.gpsimd.memset(w3_planes[:].rearrange("p g n -> p (g n)").bitcast(I32), 0)
 
-        x_raw = []
-        for c in range(CHUNKS):
-            xr = keep.tile([P, TILES * K1], U8, name=f"x_raw{c}", align_bytes=64)
-            x_raw.append(xr)
+        x_factor = keep.tile([P, X_PASSES * PACK], F32, name="x_factor", align_bytes=64)
+        nc.scalar.dma_start(
+            out=x_factor[:].rearrange("p (g s) -> p g s", s=PACK),
+            in_=x_scale.rearrange("o (g p s) -> p (o g) s", p=P, s=PACK),
+        )
+
+        x_codes = {}
+        w11_raw = {}
+        w3 = keep.tile([P, GROUPS, 2 * LATENT], I32, name="w3", align_bytes=64)
+        noise = keep.tile([P, CHUNKS, CHUNK_TILES, LATENT], BF16, name="noise", align_bytes=64)
 
         def load_x(c):
+            x_codes[c] = keep.tile([P, CHUNK_TILES * PIXELS], U8, name=f"x_codes{c}", align_bytes=64)
             nc.sync.dma_start(
-                out=x_raw[c][:],
-                in_=x_bytes[c * CHUNK : (c + 1) * CHUNK, :].rearrange("(p a) k -> p (a k)", a=TILES),
+                out=x_codes[c][:],
+                in_=x_bytes[c * CHUNK : (c + 1) * CHUNK, :].rearrange("(p a) k -> p (a k)", a=CHUNK_TILES),
             )
-
-        w11_raw = {}
-        w11 = {}
 
         def load_w11(i):
-            gid = GROUP_ORDER[i]
-            raw = work.tile([P, X_PASSES, K_PASS], I32, name="w11_raw", bufs=8, align_bytes=64)
-            w11_raw[i] = raw
+            channels = slice(GROUP_ORDER[i] * K_PASS, (GROUP_ORDER[i] + 1) * K_PASS)
+            w11_raw[i] = work.tile([P, X_PASSES, K_PASS], I32, name="w11_raw", bufs=GROUPS, align_bytes=64)
             nc.sync.dma_start(
-                out=raw[:],
-                in_=w11_words[:, :, gid * K_PASS : (gid + 1) * K_PASS, :]
-                .rearrange("g p n t -> p g (n t)")
-                .bitcast(I32),
+                out=w11_raw[i][:],
+                in_=w11_words[:, :, channels, :].rearrange("g p n s -> p g (n s)").bitcast(I32),
             )
 
-        scale_col = keep.tile([P, X_PASSES * PACK], F32, name="scale_col", align_bytes=64)
-        nc.scalar.dma_start(
-            out=scale_col[:].rearrange("p (g t) -> p g t", t=PACK),
-            in_=x_scale.rearrange("o (g p t) -> p (o g) t", p=P, t=PACK),
-        )
+        def load_w11_scales():
+            for h in range(2):
+                for q in range(4):
+                    row = 32 * q + 8 * h
+                    nc.sync.dma_start(
+                        out=w11_planes_raw[row : row + 8, :].bitcast(I32),
+                        in_=w11_scales[:, 4 * q : 4 * q + 4, h * HALF_HIDDEN : (h + 1) * HALF_HIDDEN].bitcast(I32),
+                    )
+
         load_x(0)
-        for h in range(2):
-            for q in range(4):
-                nc.sync.dma_start(
-                    out=w11s_raw[32 * q + 8 * h : 32 * q + 8 * h + 8, :].bitcast(I32),
-                    in_=w11_scales[:, 4 * q : 4 * q + 4, h * 2048 : (h + 1) * 2048].bitcast(I32),
-                )
         load_w11(0)
-        nc.sync.dma_start(out=small[0:GROUPS, 0:K_PASS], in_=b11.rearrange("(g n) -> g n", g=GROUPS))
-        load_w11(1)
+        load_w11_scales()
+        nc.sync.dma_start(out=bias_rows[0:GROUPS, 0:K_PASS], in_=b11.rearrange("(g n) -> g n", g=GROUPS))
         load_x(1)
+        load_w11(1)
         load_w11(2)
+        load_x(2)
         load_w11(3)
-        nc.sync.dma_start(out=small[0:1, 512:640], in_=b31.rearrange("(o n) -> o n", o=1))
-        nc.sync.dma_start(out=small[0:1, 640:768], in_=b32.rearrange("(o n) -> o n", o=1))
-        w3 = keep.tile([P, GROUPS, 2 * LATENT], I32, name="w3", align_bytes=64)
+        for j, bias in enumerate((b31, b32)):
+            first = K_PASS + j * LATENT
+            nc.sync.dma_start(out=bias_rows[0:1, first : first + LATENT], in_=bias.rearrange("(o n) -> o n", o=1))
+        load_w11(4)
         for j, scales in enumerate((w31_scales, w32_scales)):
-            cols = slice(j * LATENT, (j + 1) * LATENT)
             for q in range(4):
                 nc.sync.dma_start(
-                    out=w3s[32 * q : 32 * q + 4, :, cols].bitcast(I32),
+                    out=w3_planes[32 * q : 32 * q + 4, :, j * LATENT : (j + 1) * LATENT].bitcast(I32),
                     in_=scales[:, 4 * q : 4 * q + 4, :].rearrange("g q n -> q g n").bitcast(I32),
                 )
         for j, words in enumerate((w31_words, w32_words)):
             nc.sync.dma_start(
                 out=w3[:, :, j * LATENT : (j + 1) * LATENT],
-                in_=words.rearrange("g p n t -> p g (n t)").bitcast(I32),
+                in_=words.rearrange("g p n s -> p g (n s)").bitcast(I32),
             )
-        load_w11(4)
-        load_x(2)
-        load_w11(5)
         load_x(3)
+        load_w11(5)
         load_w11(6)
         load_w11(7)
-        noise = keep.tile([P, CHUNKS, TILES, LATENT], BF16, name="noise", align_bytes=64)
         for c in range(CHUNKS):
             nc.sync.dma_start(
                 out=noise[:, c, :, :],
-                in_=eps[c * CHUNK : (c + 1) * CHUNK, :].rearrange("(p a) n -> p a n", a=TILES),
+                in_=eps[c * CHUNK : (c + 1) * CHUNK, :].rearrange("(p a) n -> p a n", a=CHUNK_TILES),
             )
 
         xq = []
-        xs = []
-        for s in range(CHUNKS // 2):
-            xq_s = keep.tile([P, X_PASSES, 2 * CHUNK], U32, name=f"xq{s}", align_bytes=64)
-            xs_s = keep.tile([P, X_PASSES, 2 * CHUNK], U8, name=f"xs{s}", align_bytes=64)
-            xq.append(xq_s)
-            xs.append(xs_s)
+        xq_planes = []
+        for half in range(2):
+            xq.append(keep.tile([P, X_PASSES, HALF_TILES * P], U32, name=f"xq{half}", align_bytes=64))
+            xq_planes.append(keep.tile([P, X_PASSES, HALF_TILES * P], U8, name=f"xq_planes{half}", align_bytes=64))
         x_wide = {}
         x_bank = {}
         x_grouped = {}
 
-        def widen_tile(c):
-            xw = work.tile([P, TILES, K1], BF16, name="x_wide", bufs=2, align_bytes=64)
-            x_wide[c] = xw
+        def new_x_wide(c):
+            x_wide[c] = work.tile([P, CHUNK_TILES, PIXELS], BF16, name="x_wide", align_bytes=64)
 
-        def widen_first(c):
-            widen_tile(c)
-            for a in range(TILES):
-                for g, copy in ((0, nc.vector.tensor_copy), (1, nc.scalar.copy)):
-                    lo = a * K1 + g * K_PASS
-                    copy(
-                        out=x_wide[c][:, a, g * K_PASS : (g + 1) * K_PASS],
-                        in_=x_raw[c][:, lo : lo + K_PASS].bitcast(FP8),
-                    )
-
-        def widen(c, a):
-            copy = nc.vector.tensor_copy if c in CAST_ON_VECTOR else nc.scalar.copy
-            copy(out=x_wide[c][:, a, :], in_=x_raw[c][:, a * K1 : (a + 1) * K1].bitcast(FP8))
+        def cast_x(copy, c, a, first=0, count=PIXELS):
+            lo = a * PIXELS + first
+            copy(out=x_wide[c][:, a, first : first + count], in_=x_codes[c][:, lo : lo + count].bitcast(FP8))
 
         def turn_x(c, g):
+            bank = psum.tile([P, 2, CHUNK], F32, name="bank", bufs=4)
+            x_bank[c, g] = bank
             words = x_wide[c][:].rearrange("p a k -> p (a k)").bitcast(F32)
-            per_bank = 1 if (c, g) in SHARED else 2
-            x_bank[c, g] = []
-            for u0 in range(0, 2, per_bank):
-                bank = psum.tile([P, per_bank, CHUNK], F32, name="bank", bufs=4)
-                x_bank[c, g].append(bank)
-                for a in range(TILES):
-                    for u in range(u0, u0 + per_bank):
-                        lo = a * (K1 // 2) + g * (K_PASS // 2)
-                        nc.tensor.transpose(
-                            bank[:, u - u0, a * P : (a + 1) * P],
-                            words[:, lo + u : lo + K_PASS // 2 : 2],
-                            ident[:],
-                        )
-
-        def bank_values(bank, pairs):
-            return bank[:].rearrange("p u r -> p (u r)").bitcast(BF16).rearrange("p (u r e) -> p r u e", u=pairs, e=2)
+            for a in range(CHUNK_TILES):
+                lo = (a * PIXELS + g * K_PASS) // 2
+                for u in range(2):
+                    nc.tensor.transpose(
+                        bank[:, u, a * P : (a + 1) * P], words[:, lo + u : lo + K_PASS // 2 : 2], ident[:]
+                    )
 
         def scale_x(c, g):
             grouped = work.tile([P, CHUNK, PACK], BF16, name="x_grouped", bufs=4, align_bytes=64)
             x_grouped[c, g] = grouped
-            pairs = 1 if (c, g) in SHARED else 2
-            slots = grouped[:].rearrange("p r (u e) -> p r u e", u=2)
-            factor = scale_col[:, g * PACK : g * PACK + 2 * pairs].rearrange("p (u e) -> p u e", u=pairs)
+            values = x_bank[c, g][:].rearrange("p u r -> p (u r)").bitcast(BF16)
+            factor = x_factor[:, g * PACK : (g + 1) * PACK].rearrange("p (u e) -> p u e", u=2)
             nc.vector.tensor_tensor(
-                out=slots[:, :, 0:pairs, :],
-                in0=bank_values(x_bank[c, g][0], pairs),
-                in1=factor.unsqueeze(1).to_broadcast([P, CHUNK, pairs, 2]),
+                out=grouped[:].rearrange("p r (u e) -> p r u e", u=2),
+                in0=values.rearrange("p (u r e) -> p r u e", u=2, e=2),
+                in1=factor.unsqueeze(1).to_broadcast([P, CHUNK, 2, 2]),
                 op=ALU.mult,
             )
-            if pairs == 1:
-                for e in range(2):
-                    nc.scalar.activation(
-                        out=slots[:, :, 1, e],
-                        in_=bank_values(x_bank[c, g][1], 1)[:, :, 0, e],
-                        func=ACT.Copy,
-                        scale=scale_col[:, g * PACK + 2 + e : g * PACK + 3 + e],
-                    )
 
         def quantize_x(c, g):
-            cols = slice((c % 2) * CHUNK, (c % 2 + 1) * CHUNK)
+            half, lo = divmod(c * CHUNK, HALF_TILES * P)
             nc.vector.quantize_mx(
-                out=xq[c // 2][:, g, cols].bitcast(FP8X4),
-                scales=xs[c // 2][:, g, cols],
-                in_=x_grouped[c, g][:].rearrange("p r t -> p (r t)"),
+                out=xq[half][:, g, lo : lo + CHUNK].bitcast(FP8X4),
+                scales=xq_planes[half][:, g, lo : lo + CHUNK],
+                in_=x_grouped[c, g][:].rearrange("p r s -> p (r s)"),
             )
+
+        w11 = {}
 
         def permute_w11(i):
-            codes = keep.tile([P, PACK, X_PASSES, P], I32, name=f"w11_{i}", align_bytes=64)
-            w11[i] = codes
+            w11[i] = keep.tile([P, PACK, X_PASSES, P], I32, name=f"w11_{i}", align_bytes=64)
             nc.vector.tensor_copy(
-                out=codes[:].rearrange("p t g (c i) -> p (g c) t i", i=4),
-                in_=w11_raw[i][:].rearrange("p g (c i t) -> p (g c) t i", i=4, t=PACK),
+                out=w11[i][:].rearrange("p t g (c m) -> p (g c) t m", m=4),
+                in_=w11_raw[i][:].rearrange("p g (c m t) -> p (g c) t m", m=4, t=PACK),
             )
 
-        def permute_scales(b, engine):
-            cols = slice(b * K_PASS, (b + 1) * K_PASS)
-            engine.tensor_copy(
-                out=w11s[:, cols].rearrange("p (t m) -> p m t", t=PACK),
-                in_=w11s_raw[:, cols].rearrange("p (m t) -> p m t", t=PACK),
+        def permute_w11_scales(i):
+            cols = slice(i * K_PASS, (i + 1) * K_PASS)
+            nc.vector.tensor_copy(
+                out=w11_planes[:, cols].rearrange("p (t m) -> p m t", t=PACK),
+                in_=w11_planes_raw[:, cols].rearrange("p (m t) -> p m t", t=PACK),
             )
 
-        bias11 = keep.tile([P, GROUPS, PACK], F32, name="bias11", align_bytes=64)
-        bias3 = keep.tile([P, 2 * LATENT], F32, name="bias3", align_bytes=64)
+        b11_cols = keep.tile([P, GROUPS, PACK], F32, name="b11_cols", align_bytes=64)
+        b3_tile = keep.tile([P, 2 * LATENT], F32, name="b3_tile", align_bytes=64)
 
-        def spread_biases():
+        def turn_b11():
             turned = psum.tile([P, PACK, P], BF16, name="bank", bufs=4)
             for t in range(PACK):
-                nc.tensor.transpose(turned[:, t, :], small[:, t : K_PASS : PACK], ident_bf[:])
-            nc.scalar.copy(out=bias11[:], in_=turned[:, :, 0:GROUPS].rearrange("p t g -> p g t"))
+                nc.tensor.transpose(turned[:, t, :], bias_rows[:, t:K_PASS:PACK], ident_bf16[:])
+            nc.scalar.copy(out=b11_cols[:], in_=turned[:, :, 0:GROUPS].rearrange("p t g -> p g t"))
 
-        def spread_last_biases():
-            spread = psum.tile([P, 2, CHUNK], F32, name="bank", bufs=4)
-            nc.tensor.matmul(spread[:, 0, :], lhsT=ones[:], rhs=small[:, 512:768], start=True, stop=True)
-            nc.scalar.copy(out=bias3[:], in_=spread[:, 0, :])
+        def spread_b3():
+            spread = psum.tile([P, 2 * LATENT], F32, name="bank", bufs=4)
+            nc.tensor.matmul(
+                spread[:], lhsT=ones[:, 0:P], rhs=bias_rows[:, K_PASS : K_PASS + 2 * LATENT], start=True, stop=True
+            )
+            nc.scalar.copy(out=b3_tile[:], in_=spread[:])
+
+        unread = psum.tile([P, 2 * LATENT], F32, name=f"sums{HALF_TILES - 1}", bufs=1)
+
+        def warm_up(count):
+            for i in range(count):
+                nc.tensor.matmul(unread[:], lhsT=ones[:, 0:P], rhs=ones[:], start=True, stop=True)
 
         enc = {}
-        grouped_enc = {}
-        codes_enc = {}
-        acc = {}
+        enc_grouped = {}
+        enc_codes = {}
+        sums = {}
 
-        def paired(u):
-            return u in PAIRED
-
-        def unit_cols(u):
+        def multiply_first(u, between):
             first, tiles, i = UNITS[u]
-            lo = (first % 4) * P
-            return slice(lo, lo + tiles * P)
-
-        def multiply1(u, fillers=()):
-            fillers = list(fillers)
-            first, tiles, i = UNITS[u]
-            s = first // 4
+            group = GROUP_ORDER[i]
             n = tiles * P
-            cols = unit_cols(u)
-            gid = GROUP_ORDER[i]
-            e = work.tile([P, PACK * n], BF16, name="enc", bufs=8, align_bytes=64)
-            enc[u] = e
-            if paired(u):
-                slots = e[:].rearrange("p (h n l) -> p h l n", h=2, l=2)
-            else:
-                slots = e[:].rearrange("p (h l n) -> p h l n", h=2, l=2)
-            per_bank = min(512 // n, 2)
-            for t in range(PACK):
-                if t % per_bank == 0:
-                    bank = psum.tile([P, per_bank, n], F32, name="bank", bufs=4)
-                for g in range(X_PASSES):
-                    plane = 8 * (gid // 4) + 4 * g
-                    sc = (gid % 4) * K_PASS + t * P
-                    nc.tensor.matmul_mx(
-                        out=bank[:, t % per_bank, :],
-                        lhsT=w11[i][:, t, g, :].bitcast(FP8X4),
-                        lhsT_scale=w11s[plane:P, sc : sc + P],
-                        rhs=xq[s][:, g, cols].bitcast(FP8X4),
-                        rhs_scale=xs[s][:, g, cols],
-                        start=(g == 0),
-                        stop=(g == X_PASSES - 1),
-                    )
-                if t % per_bank == per_bank - 1:
-                    for b in range(per_bank):
-                        v = t - per_bank + 1 + b
-                        if u in TAIL_VECTOR and t == PACK - 1:
-                            nc.vector.tensor_scalar(
-                                out=slots[:, v // 2, v % 2, :],
-                                in0=bank[:, b, :],
-                                scalar1=bias11[:, gid, v : v + 1],
-                                scalar2=0.0,
-                                op0=ALU.add,
-                                op1=ALU.max,
-                            )
-                            continue
-                        nc.scalar.activation(
-                            out=slots[:, v // 2, v % 2, :],
-                            in_=bank[:, b, :],
-                            func=ACT.Relu,
-                            bias=bias11[:, gid, v : v + 1],
+            half, lo = divmod(first * P, HALF_TILES * P)
+            tokens = slice(lo, lo + n)
+            enc[u] = work.tile([P, PACK, n], BF16, name="enc", bufs=8, align_bytes=64)
+            per_bank = BANK // n
+            banks = PACK // per_bank
+            for b in range(banks):
+                bank = psum.tile([P, per_bank, n], F32, name="bank", bufs=4)
+                products = range(b * per_bank, (b + 1) * per_bank)
+                for t in products:
+                    for g in range(X_PASSES):
+                        plane = 8 * (group // 4) + 4 * g
+                        cols = slice((group % 4) * K_PASS + t * P, (group % 4) * K_PASS + (t + 1) * P)
+                        nc.tensor.matmul_mx(
+                            out=bank[:, t % per_bank, :],
+                            lhsT=w11[i][:, t, g, :].bitcast(FP8X4),
+                            lhsT_scale=w11_planes[plane:P, cols],
+                            rhs=xq[half][:, g, tokens].bitcast(FP8X4),
+                            rhs_scale=xq_planes[half][:, g, tokens],
+                            start=(g == 0),
+                            stop=(g == X_PASSES - 1),
                         )
-                    banks_left = (PACK - 1 - t) // per_bank
-                    while len(fillers) > banks_left * ((len(fillers) + banks_left) // (banks_left + 1)):
-                        fillers.pop(0)()
-            for filler in fillers:
-                filler()
+                for t in products:
+                    nc.scalar.activation(
+                        out=enc[u][:, t, :],
+                        in_=bank[:, t % per_bank, :],
+                        func=ACT.Relu,
+                        bias=b11_cols[:, group, t : t + 1],
+                    )
+                for call in between[b * len(between) // banks : (b + 1) * len(between) // banks]:
+                    call()
 
         def interleave(u):
             n = UNITS[u][1] * P
-            grouped = work.tile([P, n, PACK], BF16, name="enc_grouped", bufs=3, align_bytes=64)
-            grouped_enc[u] = grouped
-            if paired(u):
-                nc.vector.tensor_copy(
-                    out=grouped[:].rearrange("p n t -> p (n t)").bitcast(F32),
-                    in_=enc[u][:].bitcast(F32).rearrange("p (h n) -> p n h", h=2),
-                )
-            else:
-                copy = nc.scalar.copy if u in ON_SCALAR else nc.vector.tensor_copy
-                copy(
-                    out=grouped[:].rearrange("p (c i) t -> p c t i", i=4),
-                    in_=enc[u][:].rearrange("p (t c i) -> p c t i", t=PACK, i=4),
-                )
+            enc_grouped[u] = work.tile([P, n, PACK], BF16, name="enc_grouped", bufs=3, align_bytes=64)
+            nc.vector.tensor_copy(
+                out=enc_grouped[u][:].rearrange("p (c r) t -> p c t r", r=4),
+                in_=enc[u][:].rearrange("p t (c r) -> p c t r", r=4),
+            )
 
         def quantize(u):
             n = UNITS[u][1] * P
             codes = work.tile([P, n], U32, name="enc_codes", bufs=7, align_bytes=64)
             planes = work.tile([P, n], U8, name="enc_planes", bufs=7, align_bytes=64)
-            codes_enc[u] = (codes, planes)
+            enc_codes[u] = (codes, planes)
             nc.vector.quantize_mx(
                 out=codes[:].bitcast(FP8X4),
                 scales=planes[:],
-                in_=grouped_enc[u][:].rearrange("p r t -> p (r t)"),
+                in_=enc_grouped[u][:].rearrange("p r t -> p (r t)"),
             )
 
-        def multiply2(u):
-            return [lambda b=b: multiply2_tile(u, b) for b in range(UNITS[u][1])]
-
-        def multiply2_tile(u, b):
+        def multiply_second(u, b):
             first, tiles, i = UNITS[u]
             tile = first + b
-            gid = GROUP_ORDER[i]
-            codes, planes = codes_enc[u]
             if i == 0:
-                sums = psum.tile([P, 2 * LATENT], F32, name=f"sums{tile % 4}", bufs=1)
-                acc[tile] = sums
-            cols = slice(b * P, (b + 1) * P)
+                sums[tile] = psum.tile([P, 2 * LATENT], F32, name=f"sums{tile % HALF_TILES}", bufs=1)
+            codes, planes = enc_codes[u]
+            tokens = slice(b * P, (b + 1) * P)
             nc.tensor.matmul_mx(
-                out=acc[tile][:],
-                lhsT=codes[:, cols].bitcast(FP8X4),
-                lhsT_scale=planes[:, cols],
-                rhs=w3[:, gid, :].bitcast(FP8X4),
-                rhs_scale=w3s[:, gid, :],
+                out=sums[tile][:],
+                lhsT=codes[:, tokens].bitcast(FP8X4),
+                lhsT_scale=planes[:, tokens],
+                rhs=w3[:, GROUP_ORDER[i], :].bitcast(FP8X4),
+                rhs_scale=w3_planes[:, GROUP_ORDER[i], :],
                 start=(i == 0),
                 stop=(i == GROUPS - 1),
             )
-            if i == GROUPS - 1 and b == tiles - 1:
-                ready.append((first, tiles))
 
-        later = []
+        endings = []
 
-        def finish(first, tiles):
-            for lo in range(first, first + tiles, TILES):
-                finish_tiles(lo // TILES, lo % TILES, min(TILES, tiles))
+        def finish(c):
+            pre = work.tile([P, CHUNK_TILES, 2, LATENT], F32, name="pre", bufs=3, align_bytes=64)
+            both = work.tile([P, 2, CHUNK_TILES, LATENT], F32, name="both", bufs=3, align_bytes=64)
+            z = work.tile([P, CHUNK_TILES, LATENT], F32, name="z", bufs=3, align_bytes=64)
+            rows = slice(c * CHUNK, (c + 1) * CHUNK)
 
-        def finish_tiles(c, a0, tiles):
-            pre = work.tile([P, tiles, 2, LATENT], F32, name="pre", bufs=3, align_bytes=64)
-            both = work.tile([P, 2, tiles, LATENT], F32, name="both", bufs=3, align_bytes=64)
-            z = work.tile([P, tiles, LATENT], F32, name="z", bufs=3, align_bytes=64)
-            for a in range(tiles):
+            def store(result, tile):
+                nc.sync.dma_start(out=result[rows, :].rearrange("(p a) n -> p a n", a=CHUNK_TILES), in_=tile)
+
+            for a in range(CHUNK_TILES):
                 nc.vector.tensor_tensor(
-                    out=pre[:, a, :, :].rearrange("p w n -> p (w n)"),
-                    in0=acc[c * TILES + a0 + a][:],
-                    in1=bias3[:],
+                    out=pre[:, a, :, :].rearrange("p j n -> p (j n)"),
+                    in0=sums[c * CHUNK_TILES + a][:],
+                    in1=b3_tile[:],
                     op=ALU.add,
                 )
-            if c in RELU_ON_GPSIMD:
-                for a in range(tiles):
+            if c < CHUNKS // 2:
+                for a in range(CHUNK_TILES):
                     nc.gpsimd.tensor_scalar(
                         out=both[:, :, a, :], in0=pre[:, a, :, :], scalar1=0.0, scalar2=0.0, op0=ALU.max, op1=ALU.add
                     )
             else:
-                nc.scalar.activation(out=both[:].rearrange("p w a n -> p a w n"), in_=pre[:], func=ACT.Relu)
-            def weigh():
+                nc.scalar.activation(out=both[:].rearrange("p j a n -> p a j n"), in_=pre[:], func=ACT.Relu)
+            store(out_mu, both[:, 0, :, :])
+            store(out_sigma, both[:, 1, :, :])
+
+            def times_noise():
                 nc.vector.scalar_tensor_tensor(
-                    out=z[:], in0=pre[:, :, 1, :], scalar=0.0, in1=noise[:, c, a0 : a0 + tiles, :], op0=ALU.max, op1=ALU.mult
+                    out=z[:], in0=pre[:, :, 1, :], scalar=0.0, in1=noise[:, c, :, :], op0=ALU.max, op1=ALU.mult
                 )
 
-            def shift():
+            def plus_mu():
                 nc.vector.scalar_tensor_tensor(
                     out=z[:], in0=pre[:, :, 0, :], scalar=0.0, in1=z[:], op0=ALU.max, op1=ALU.add
                 )
                 store(out_z, z[:])
 
-            rows = slice(c * CHUNK, (c + 1) * CHUNK)
+            endings.extend((times_noise, plus_mu))
 
-            def store(dst, src):
-                nc.sync.dma_start(
-                    out=dst[rows, :].rearrange("(p a) n -> p a n", a=TILES)[:, a0 : a0 + tiles, :], in_=src
-                )
-
-            store(out_mu, both[:, 0, :, :])
-            store(out_sigma, both[:, 1, :, :])
-            later.extend((weigh, shift))
-
-        widen_first(0)
-        turn_x(0, 0)
-        turn_x(0, 1)
-        scale_x(0, 0)
-        scale_x(0, 1)
-        spread_biases()
-        widen_tile(1)
-        widen(1, 0)
-        widen(1, 1)
-        quantize_x(0, 0)
-        quantize_x(0, 1)
+        new_x_wide(0)
+        for a in range(CHUNK_TILES):
+            cast_x(nc.vector.tensor_copy, 0, a, 0, K_PASS)
+            cast_x(nc.scalar.copy, 0, a, K_PASS, K_PASS)
+        for g in range(X_PASSES):
+            turn_x(0, g)
         permute_w11(0)
-        permute_scales(0, nc.vector)
+        for g in range(X_PASSES):
+            scale_x(0, g)
+        warm_up(WARM_BEFORE)
+        turn_b11()
+        warm_up(WARM_AFTER)
+        new_x_wide(1)
+        for a in range(CHUNK_TILES):
+            cast_x(nc.scalar.copy, 1, a)
+        for g in range(X_PASSES):
+            quantize_x(0, g)
+        permute_w11_scales(0)
         permute_w11(1)
-        permute_scales(1, nc.vector)
-        before = {5: [spread_last_biases]}
-        def put(k, item):
-            before.setdefault(k, []).append(item)
+        permute_w11_scales(1)
 
-        for c in (1, 2, 3):
-            k = X_STEP[c]
-            if c > 1:
-                put(k - 2, lambda c=c: widen_tile(c))
-                put(k - 2, lambda c=c: widen(c, 0))
-                put(k - 1, lambda c=c: widen(c, 1))
-            for g in range(X_PASSES):
-                put(k, lambda c=c, g=g: turn_x(c, g))
-            for g in range(X_PASSES):
-                put(k, lambda c=c, g=g: scale_x(c, g))
-            for g in range(X_PASSES):
-                put(k + 1, lambda c=c, g=g: quantize_x(c, g))
-        first_use = {}
-        for u, (first, tiles, i) in enumerate(UNITS):
-            first_use.setdefault(i, u)
-        for i in range(2, GROUPS):
-            put(first_use[i] - PERM_AHEAD, lambda i=i: permute_w11(i))
-            if i in (2, 3):
-                put(first_use[i] - PERM_AHEAD, lambda i=i: permute_scales(i, nc.vector))
-        ready = []
-        made = [0, 0, 0]
-        for k in range(len(UNITS) + 4):
-            lags = LAGS if k < LATE else LATE_LAGS
-            for work_item in before.get(k, []):
-                work_item()
-            while made[1] < len(UNITS) and made[1] <= k - lags[1] or made[0] < len(UNITS) and made[0] <= k - lags[0]:
-                if made[0] < len(UNITS) and made[0] <= k - lags[0]:
-                    interleave(made[0])
-                    made[0] += 1
-                    if later:
-                        later.pop(0)()
-                if made[1] < len(UNITS) and made[1] <= k - lags[1]:
-                    quantize(made[1])
-                    made[1] += 1
-                    if later:
-                        later.pop(0)()
-            fillers = []
-            while made[2] < len(UNITS) and made[2] <= k - lags[2]:
-                fillers += multiply2(made[2])
-                made[2] += 1
-            if k < len(UNITS):
-                multiply1(k, fillers)
-            else:
-                for filler in fillers:
-                    filler()
-            for first, tiles in ready:
-                finish(first, tiles)
-            ready.clear()
-        for work_item in later:
-            work_item()
+        def prepare(k):
+            if k == BIAS_STEP:
+                spread_b3()
+            for c, step in X_STEP.items():
+                if c > 1 and k == step - 2:
+                    new_x_wide(c)
+                if c > 1 and k in (step - 2, step - 1):
+                    cast_x(nc.vector.tensor_copy if c == 2 else nc.scalar.copy, c, k - step + 2)
+                if k == step:
+                    for g in range(X_PASSES):
+                        turn_x(c, g)
+                    for g in range(X_PASSES):
+                        scale_x(c, g)
+                if k == step + 1:
+                    for g in range(X_PASSES):
+                        quantize_x(c, g)
+            if k + 1 < len(UNITS):
+                i = UNITS[k + 1][2]
+                if i not in w11:
+                    permute_w11(i)
+                    if i < GROUPS // 2:
+                        permute_w11_scales(i)
+
+        def reshape_enc(interleaved, quantized):
+            while len(enc_grouped) < interleaved or len(enc_codes) < quantized:
+                if len(enc_grouped) < interleaved:
+                    interleave(len(enc_grouped))
+                    if endings:
+                        endings.pop(0)()
+                if len(enc_codes) < quantized:
+                    quantize(len(enc_codes))
+                    if endings:
+                        endings.pop(0)()
+
+        def finished_by(u):
+            first, tiles, i = UNITS[u]
+            return range(first // CHUNK_TILES, (first + tiles) // CHUNK_TILES) if i == GROUPS - 1 else ()
+
+        def second_calls(u):
+            return [lambda b=b: multiply_second(u, b) for b in range(UNITS[u][1])]
+
+        for k in range(len(UNITS)):
+            prepare(k)
+            reshape_enc(k - INTERLEAVE_LAG + 1, k - QUANTIZE_LAG + 1)
+            if k > SECOND_LAG:
+                for c in finished_by(k - SECOND_LAG - 1):
+                    finish(c)
+            multiply_first(k, second_calls(k - SECOND_LAG) if k >= SECOND_LAG else [])
+
+        reshape_enc(len(UNITS), len(UNITS))
+        for u in range(len(UNITS) - SECOND_LAG, len(UNITS)):
+            for call in second_calls(u):
+                call()
+        for u in range(len(UNITS) - SECOND_LAG - 1, len(UNITS)):
+            for c in finished_by(u):
+                finish(c)
+        for ending in endings[0::2] + endings[1::2]:
+            ending()

from contextlib import ExitStack

import concourse.mybir as mybir
from concourse.masks import make_identity

F32 = mybir.dt.float32
BF16 = mybir.dt.bfloat16
I32 = mybir.dt.int32
U32 = mybir.dt.uint32
U8 = mybir.dt.uint8
FP8 = mybir.dt.float8_e4m3fn
FP8X4 = mybir.dt.float8_e4m3fn_x4
ACT = mybir.ActivationFunctionType
ALU = mybir.AluOpType

TOKENS, PIXELS, HIDDEN, LATENT = 1024, 1024, 4096, 128
FLOPS = 2 * TOKENS * PIXELS * HIDDEN + 2 * TOKENS * HIDDEN * 2 * LATENT

P = 128
PACK = 4
K_PASS = P * PACK
X_PASSES = PIXELS // K_PASS
GROUPS = HIDDEN // K_PASS
CHUNK_TILES = 2
CHUNK = CHUNK_TILES * P
CHUNKS = TOKENS // CHUNK
HALF_TILES = 4
BANK = 512

HALF_HIDDEN = HIDDEN // 2
GROUP_ORDER = (0, 4, 1, 5, 2, 6, 3, 7)

UNITS = (
    [(0, 2, 0), (0, 2, 1), (2, 2, 0), (2, 2, 1)]
    + [(0, 4, i) for i in range(2, GROUPS)]
    + [(4, 2, 0), (6, 2, 0)]
    + [(4, 4, i) for i in range(1, GROUPS - 1)]
    + [(4, 2, GROUPS - 1), (6, 2, GROUPS - 1)]
)
INTERLEAVE_LAG, QUANTIZE_LAG, SECOND_LAG = 2, 3, 5
X_STEP = {1: 0, 2: 6, 3: 9}
BIAS_STEP = 5
WARM_BEFORE, WARM_AFTER = 3, 5


def tile_mae_pa_w8_kernel(
    tc,
    x_bytes,
    x_scale,
    eps,
    w11_words,
    w11_scales,
    b11,
    w31_words,
    w31_scales,
    b31,
    w32_words,
    w32_scales,
    b32,
    out_mu,
    out_sigma,
    out_z,
):
    nc = tc.nc
    with ExitStack() as ctx:
        keep = ctx.enter_context(tc.tile_pool(name="keep", bufs=1))
        work = ctx.enter_context(tc.tile_pool(name="work", bufs=2))
        psum = ctx.enter_context(tc.psum_pool(name="psum", bufs=1))
        ctx.enter_context(tc.manual_schedule())

        first_act = keep.tile([P, 1], F32, name="first_act")
        nc.vector.memset(first_act[:], 0.0)
        nc.scalar.activation(out=first_act[:], in_=first_act[:], func=ACT.Relu)

        w11_planes_raw = keep.tile([P, HALF_HIDDEN], U8, name="w11_planes_raw", align_bytes=64)
        w11_planes = keep.tile([P, HALF_HIDDEN], U8, name="w11_planes", align_bytes=64)
        nc.vector.memset(w11_planes_raw[:].bitcast(I32), 0)
        bias_rows = keep.tile([P, K_PASS + 2 * LATENT], BF16, name="bias_rows", align_bytes=64)
        nc.vector.memset(bias_rows[:], 0.0)
        ones = keep.tile([P, 2 * LATENT], BF16, name="ones", align_bytes=64)
        nc.vector.memset(ones[:], 1.0)
        ident = keep.tile([P, P], F32, name="ident", align_bytes=64)
        make_identity(nc, ident[:])
        ident_bf16 = keep.tile([P, P], BF16, name="ident_bf16", align_bytes=64)
        make_identity(nc, ident_bf16[:])
        w3_planes = keep.tile([P, GROUPS, 2 * LATENT], U8, name="w3_planes", align_bytes=64)
        nc.gpsimd.memset(w3_planes[:].rearrange("p g n -> p (g n)").bitcast(I32), 0)

        x_factor = keep.tile([P, X_PASSES * PACK], F32, name="x_factor", align_bytes=64)
        nc.scalar.dma_start(
            out=x_factor[:].rearrange("p (g s) -> p g s", s=PACK),
            in_=x_scale.rearrange("o (g p s) -> p (o g) s", p=P, s=PACK),
        )

        x_codes = {}
        w11_raw = {}
        w3 = keep.tile([P, GROUPS, 2 * LATENT], I32, name="w3", align_bytes=64)
        noise = keep.tile([P, CHUNKS, CHUNK_TILES, LATENT], BF16, name="noise", align_bytes=64)

        def load_x(c):
            x_codes[c] = keep.tile([P, CHUNK_TILES * PIXELS], U8, name=f"x_codes{c}", align_bytes=64)
            nc.sync.dma_start(
                out=x_codes[c][:],
                in_=x_bytes[c * CHUNK : (c + 1) * CHUNK, :].rearrange("(p a) k -> p (a k)", a=CHUNK_TILES),
            )

        def load_w11(i):
            channels = slice(GROUP_ORDER[i] * K_PASS, (GROUP_ORDER[i] + 1) * K_PASS)
            w11_raw[i] = work.tile([P, X_PASSES, K_PASS], I32, name="w11_raw", bufs=GROUPS, align_bytes=64)
            nc.sync.dma_start(
                out=w11_raw[i][:],
                in_=w11_words[:, :, channels, :].rearrange("g p n s -> p g (n s)").bitcast(I32),
            )

        def load_w11_scales():
            for h in range(2):
                for q in range(4):
                    row = 32 * q + 8 * h
                    nc.sync.dma_start(
                        out=w11_planes_raw[row : row + 8, :].bitcast(I32),
                        in_=w11_scales[:, 4 * q : 4 * q + 4, h * HALF_HIDDEN : (h + 1) * HALF_HIDDEN].bitcast(I32),
                    )

        load_x(0)
        load_w11(0)
        load_w11_scales()
        nc.sync.dma_start(out=bias_rows[0:GROUPS, 0:K_PASS], in_=b11.rearrange("(g n) -> g n", g=GROUPS))
        load_x(1)
        load_w11(1)
        load_w11(2)
        load_x(2)
        load_w11(3)
        for j, bias in enumerate((b31, b32)):
            first = K_PASS + j * LATENT
            nc.sync.dma_start(out=bias_rows[0:1, first : first + LATENT], in_=bias.rearrange("(o n) -> o n", o=1))
        load_w11(4)
        for j, scales in enumerate((w31_scales, w32_scales)):
            for q in range(4):
                nc.sync.dma_start(
                    out=w3_planes[32 * q : 32 * q + 4, :, j * LATENT : (j + 1) * LATENT].bitcast(I32),
                    in_=scales[:, 4 * q : 4 * q + 4, :].rearrange("g q n -> q g n").bitcast(I32),
                )
        for j, words in enumerate((w31_words, w32_words)):
            nc.sync.dma_start(
                out=w3[:, :, j * LATENT : (j + 1) * LATENT],
                in_=words.rearrange("g p n s -> p g (n s)").bitcast(I32),
            )
        load_x(3)
        load_w11(5)
        load_w11(6)
        load_w11(7)
        for c in range(CHUNKS):
            nc.sync.dma_start(
                out=noise[:, c, :, :],
                in_=eps[c * CHUNK : (c + 1) * CHUNK, :].rearrange("(p a) n -> p a n", a=CHUNK_TILES),
            )

        xq = []
        xq_planes = []
        for half in range(2):
            xq.append(keep.tile([P, X_PASSES, HALF_TILES * P], U32, name=f"xq{half}", align_bytes=64))
            xq_planes.append(keep.tile([P, X_PASSES, HALF_TILES * P], U8, name=f"xq_planes{half}", align_bytes=64))
        x_wide = {}
        x_bank = {}
        x_grouped = {}

        def new_x_wide(c):
            x_wide[c] = work.tile([P, CHUNK_TILES, PIXELS], BF16, name="x_wide", align_bytes=64)

        def cast_x(copy, c, a, first=0, count=PIXELS):
            lo = a * PIXELS + first
            copy(out=x_wide[c][:, a, first : first + count], in_=x_codes[c][:, lo : lo + count].bitcast(FP8))

        def turn_x(c, g):
            bank = psum.tile([P, 2, CHUNK], F32, name="bank", bufs=4)
            x_bank[c, g] = bank
            words = x_wide[c][:].rearrange("p a k -> p (a k)").bitcast(F32)
            for a in range(CHUNK_TILES):
                lo = (a * PIXELS + g * K_PASS) // 2
                for u in range(2):
                    nc.tensor.transpose(
                        bank[:, u, a * P : (a + 1) * P], words[:, lo + u : lo + K_PASS // 2 : 2], ident[:]
                    )

        def scale_x(c, g):
            grouped = work.tile([P, CHUNK, PACK], BF16, name="x_grouped", bufs=4, align_bytes=64)
            x_grouped[c, g] = grouped
            values = x_bank[c, g][:].rearrange("p u r -> p (u r)").bitcast(BF16)
            factor = x_factor[:, g * PACK : (g + 1) * PACK].rearrange("p (u e) -> p u e", u=2)
            nc.vector.tensor_tensor(
                out=grouped[:].rearrange("p r (u e) -> p r u e", u=2),
                in0=values.rearrange("p (u r e) -> p r u e", u=2, e=2),
                in1=factor.unsqueeze(1).to_broadcast([P, CHUNK, 2, 2]),
                op=ALU.mult,
            )

        def quantize_x(c, g):
            half, lo = divmod(c * CHUNK, HALF_TILES * P)
            nc.vector.quantize_mx(
                out=xq[half][:, g, lo : lo + CHUNK].bitcast(FP8X4),
                scales=xq_planes[half][:, g, lo : lo + CHUNK],
                in_=x_grouped[c, g][:].rearrange("p r s -> p (r s)"),
            )

        w11 = {}

        def permute_w11(i):
            w11[i] = keep.tile([P, PACK, X_PASSES, P], I32, name=f"w11_{i}", align_bytes=64)
            nc.vector.tensor_copy(
                out=w11[i][:].rearrange("p t g (c m) -> p (g c) t m", m=4),
                in_=w11_raw[i][:].rearrange("p g (c m t) -> p (g c) t m", m=4, t=PACK),
            )

        def permute_w11_scales(i):
            cols = slice(i * K_PASS, (i + 1) * K_PASS)
            nc.vector.tensor_copy(
                out=w11_planes[:, cols].rearrange("p (t m) -> p m t", t=PACK),
                in_=w11_planes_raw[:, cols].rearrange("p (m t) -> p m t", t=PACK),
            )

        b11_cols = keep.tile([P, GROUPS, PACK], F32, name="b11_cols", align_bytes=64)
        b3_tile = keep.tile([P, 2 * LATENT], F32, name="b3_tile", align_bytes=64)

        def turn_b11():
            turned = psum.tile([P, PACK, P], BF16, name="bank", bufs=4)
            for t in range(PACK):
                nc.tensor.transpose(turned[:, t, :], bias_rows[:, t:K_PASS:PACK], ident_bf16[:])
            nc.scalar.copy(out=b11_cols[:], in_=turned[:, :, 0:GROUPS].rearrange("p t g -> p g t"))

        def spread_b3():
            spread = psum.tile([P, 2 * LATENT], F32, name="bank", bufs=4)
            nc.tensor.matmul(
                spread[:], lhsT=ones[:, 0:P], rhs=bias_rows[:, K_PASS : K_PASS + 2 * LATENT], start=True, stop=True
            )
            nc.scalar.copy(out=b3_tile[:], in_=spread[:])

        unread = psum.tile([P, 2 * LATENT], F32, name=f"sums{HALF_TILES - 1}", bufs=1)

        def warm_up(count):
            for i in range(count):
                nc.tensor.matmul(unread[:], lhsT=ones[:, 0:P], rhs=ones[:], start=True, stop=True)

        enc = {}
        enc_grouped = {}
        enc_codes = {}
        sums = {}

        def multiply_first(u, between):
            first, tiles, i = UNITS[u]
            group = GROUP_ORDER[i]
            n = tiles * P
            half, lo = divmod(first * P, HALF_TILES * P)
            tokens = slice(lo, lo + n)
            enc[u] = work.tile([P, PACK, n], BF16, name="enc", bufs=8, align_bytes=64)
            per_bank = BANK // n
            banks = PACK // per_bank
            for b in range(banks):
                bank = psum.tile([P, per_bank, n], F32, name="bank", bufs=4)
                products = range(b * per_bank, (b + 1) * per_bank)
                for t in products:
                    for g in range(X_PASSES):
                        plane = 8 * (group // 4) + 4 * g
                        cols = slice((group % 4) * K_PASS + t * P, (group % 4) * K_PASS + (t + 1) * P)
                        nc.tensor.matmul_mx(
                            out=bank[:, t % per_bank, :],
                            lhsT=w11[i][:, t, g, :].bitcast(FP8X4),
                            lhsT_scale=w11_planes[plane:P, cols],
                            rhs=xq[half][:, g, tokens].bitcast(FP8X4),
                            rhs_scale=xq_planes[half][:, g, tokens],
                            start=(g == 0),
                            stop=(g == X_PASSES - 1),
                        )
                for t in products:
                    nc.scalar.activation(
                        out=enc[u][:, t, :],
                        in_=bank[:, t % per_bank, :],
                        func=ACT.Relu,
                        bias=b11_cols[:, group, t : t + 1],
                    )
                for call in between[b * len(between) // banks : (b + 1) * len(between) // banks]:
                    call()

        def interleave(u):
            n = UNITS[u][1] * P
            enc_grouped[u] = work.tile([P, n, PACK], BF16, name="enc_grouped", bufs=3, align_bytes=64)
            nc.vector.tensor_copy(
                out=enc_grouped[u][:].rearrange("p (c r) t -> p c t r", r=4),
                in_=enc[u][:].rearrange("p t (c r) -> p c t r", r=4),
            )

        def quantize(u):
            n = UNITS[u][1] * P
            codes = work.tile([P, n], U32, name="enc_codes", bufs=7, align_bytes=64)
            planes = work.tile([P, n], U8, name="enc_planes", bufs=7, align_bytes=64)
            enc_codes[u] = (codes, planes)
            nc.vector.quantize_mx(
                out=codes[:].bitcast(FP8X4),
                scales=planes[:],
                in_=enc_grouped[u][:].rearrange("p r t -> p (r t)"),
            )

        def multiply_second(u, b):
            first, tiles, i = UNITS[u]
            tile = first + b
            if i == 0:
                sums[tile] = psum.tile([P, 2 * LATENT], F32, name=f"sums{tile % HALF_TILES}", bufs=1)
            codes, planes = enc_codes[u]
            tokens = slice(b * P, (b + 1) * P)
            nc.tensor.matmul_mx(
                out=sums[tile][:],
                lhsT=codes[:, tokens].bitcast(FP8X4),
                lhsT_scale=planes[:, tokens],
                rhs=w3[:, GROUP_ORDER[i], :].bitcast(FP8X4),
                rhs_scale=w3_planes[:, GROUP_ORDER[i], :],
                start=(i == 0),
                stop=(i == GROUPS - 1),
            )

        endings = []

        def finish(c):
            pre = work.tile([P, CHUNK_TILES, 2, LATENT], F32, name="pre", bufs=3, align_bytes=64)
            both = work.tile([P, 2, CHUNK_TILES, LATENT], F32, name="both", bufs=3, align_bytes=64)
            z = work.tile([P, CHUNK_TILES, LATENT], F32, name="z", bufs=3, align_bytes=64)
            rows = slice(c * CHUNK, (c + 1) * CHUNK)

            def store(result, tile):
                nc.sync.dma_start(out=result[rows, :].rearrange("(p a) n -> p a n", a=CHUNK_TILES), in_=tile)

            for a in range(CHUNK_TILES):
                nc.vector.tensor_tensor(
                    out=pre[:, a, :, :].rearrange("p j n -> p (j n)"),
                    in0=sums[c * CHUNK_TILES + a][:],
                    in1=b3_tile[:],
                    op=ALU.add,
                )
            if c < CHUNKS // 2:
                for a in range(CHUNK_TILES):
                    nc.gpsimd.tensor_scalar(
                        out=both[:, :, a, :], in0=pre[:, a, :, :], scalar1=0.0, scalar2=0.0, op0=ALU.max, op1=ALU.add
                    )
            else:
                nc.scalar.activation(out=both[:].rearrange("p j a n -> p a j n"), in_=pre[:], func=ACT.Relu)
            store(out_mu, both[:, 0, :, :])
            store(out_sigma, both[:, 1, :, :])

            def times_noise():
                nc.vector.scalar_tensor_tensor(
                    out=z[:], in0=pre[:, :, 1, :], scalar=0.0, in1=noise[:, c, :, :], op0=ALU.max, op1=ALU.mult
                )

            def plus_mu():
                nc.vector.scalar_tensor_tensor(
                    out=z[:], in0=pre[:, :, 0, :], scalar=0.0, in1=z[:], op0=ALU.max, op1=ALU.add
                )
                store(out_z, z[:])

            endings.extend((times_noise, plus_mu))

        new_x_wide(0)
        for a in range(CHUNK_TILES):
            cast_x(nc.vector.tensor_copy, 0, a, 0, K_PASS)
            cast_x(nc.scalar.copy, 0, a, K_PASS, K_PASS)
        for g in range(X_PASSES):
            turn_x(0, g)
        permute_w11(0)
        for g in range(X_PASSES):
            scale_x(0, g)
        warm_up(WARM_BEFORE)
        turn_b11()
        warm_up(WARM_AFTER)
        new_x_wide(1)
        for a in range(CHUNK_TILES):
            cast_x(nc.scalar.copy, 1, a)
        for g in range(X_PASSES):
            quantize_x(0, g)
        permute_w11_scales(0)
        permute_w11(1)
        permute_w11_scales(1)

        def prepare(k):
            if k == BIAS_STEP:
                spread_b3()
            for c, step in X_STEP.items():
                if c > 1 and k == step - 2:
                    new_x_wide(c)
                if c > 1 and k in (step - 2, step - 1):
                    cast_x(nc.vector.tensor_copy if c == 2 else nc.scalar.copy, c, k - step + 2)
                if k == step:
                    for g in range(X_PASSES):
                        turn_x(c, g)
                    for g in range(X_PASSES):
                        scale_x(c, g)
                if k == step + 1:
                    for g in range(X_PASSES):
                        quantize_x(c, g)
            if k + 1 < len(UNITS):
                i = UNITS[k + 1][2]
                if i not in w11:
                    permute_w11(i)
                    if i < GROUPS // 2:
                        permute_w11_scales(i)

        def reshape_enc(interleaved, quantized):
            while len(enc_grouped) < interleaved or len(enc_codes) < quantized:
                if len(enc_grouped) < interleaved:
                    interleave(len(enc_grouped))
                    if endings:
                        endings.pop(0)()
                if len(enc_codes) < quantized:
                    quantize(len(enc_codes))
                    if endings:
                        endings.pop(0)()

        def finished_by(u):
            first, tiles, i = UNITS[u]
            return range(first // CHUNK_TILES, (first + tiles) // CHUNK_TILES) if i == GROUPS - 1 else ()

        def second_calls(u):
            return [lambda b=b: multiply_second(u, b) for b in range(UNITS[u][1])]

        for k in range(len(UNITS)):
            prepare(k)
            reshape_enc(k - INTERLEAVE_LAG + 1, k - QUANTIZE_LAG + 1)
            if k > SECOND_LAG:
                for c in finished_by(k - SECOND_LAG - 1):
                    finish(c)
            multiply_first(k, second_calls(k - SECOND_LAG) if k >= SECOND_LAG else [])

        reshape_enc(len(UNITS), len(UNITS))
        for u in range(len(UNITS) - SECOND_LAG, len(UNITS)):
            for call in second_calls(u):
                call()
        for u in range(len(UNITS) - SECOND_LAG - 1, len(UNITS)):
            for c in finished_by(u):
                finish(c)
        for ending in endings[0::2] + endings[1::2]:
            ending()
